import numpy as np
import ml_dtypes


def mxq(x, axis, fmt="e4m3"):
    dtype, down = {"e4m3": (ml_dtypes.float8_e4m3fn, 7), "e5m2": (ml_dtypes.float8_e5m2, 14)}[fmt]
    v = np.moveaxis(np.asarray(x, np.float32).astype(ml_dtypes.bfloat16).astype(np.float64), axis, -1)
    blocks = v.reshape(v.shape[:-1] + (-1, 32))
    amax = np.abs(blocks).max(-1, keepdims=True)
    byte = np.maximum(np.where(amax > 0, np.frexp(amax)[1] - 1 + 127, 0) - down, 1)
    scale = np.exp2(byte - 127.0)
    codes = (blocks / scale).astype(np.float32).astype(dtype).astype(np.float64)
    return np.moveaxis((codes * scale).reshape(v.shape), -1, axis)


WIDE = False


def mx_kscale(k):
    if not WIDE:
        return np.ones(k)
    levels = np.array([10, -10, 5, -5, 0])
    a = np.random.permutation(np.resize(levels, k // 512 * 4)).reshape(k // 512, 4)
    idx = np.arange(k)
    return np.exp2(a[idx // 512, idx % 128 // 32])


BF16 = ml_dtypes.bfloat16


def bf(x):
    return np.asarray(x, np.float32).astype(BF16)


def f64(x):
    return np.asarray(x).astype(np.float64)


B, S, H, NH, FF = 2, 512, 1024, 8, 3072
HD = H // NH
EPS = 1e-7


def layer_norm(x, g, b):
    m = x.mean(-1, keepdims=True)
    v = ((x - m) ** 2).mean(-1, keepdims=True)
    return (x - m) / np.sqrt(v + EPS) * g + b


def erf(z):
    z = np.clip(z, -6.0, 6.0)
    z2 = 2.0 * z * z
    term = z.copy()
    total = z.copy()
    for n in range(1, 100):
        term *= z2
        term /= 2 * n + 1
        total += term
    return 2.0 / np.sqrt(np.pi) * np.exp(-z * z) * total


def gelu_erf(v):
    return 0.5 * v * (1.0 + erf(v / np.sqrt(2.0)))


def setup_inputs():
    s = mx_kscale(H)
    r = np.random.standard_normal
    return {"head_context": bf(r((B, NH, S, HD)) * 0.5 * s.reshape(NH, 1, HD)), "h": bf(r((B, S, H))),
            "Wo": bf(r((H, H)) * 2.0 / np.sqrt(H) / s[:, None]), "bo": bf(r(H) * 0.2),
            "ln1_g": bf(1.0 + 0.1 * r(H)), "ln1_b": bf(0.1 * r(H)),
            "Wi": bf(r((H, FF)) / np.sqrt(H)), "bi": bf(r(FF) * 0.2)}


def reference(head_context, h, Wo, bo, ln1_g, ln1_b, Wi, bi):
    c = f64(head_context).transpose(0, 2, 1, 3).reshape(B, S, H)
    a = layer_norm((mxq(c, 2, "e4m3") @ mxq(f64(Wo), 0, "e4m3")) + f64(bo) + f64(h), f64(ln1_g), f64(ln1_b))
    f = gelu_erf((mxq(a, 2, "e4m3") @ mxq(f64(Wi), 0, "e4m3")) + f64(bi))
    return a, f

@@ -1,0 +1,381 @@
+from contextlib import ExitStack
+
+import concourse.mybir as mybir
+from concourse.masks import make_identity
+
+F32 = mybir.dt.float32
+BF16 = mybir.dt.bfloat16
+U32 = mybir.dt.uint32
+U8 = mybir.dt.uint8
+I32 = mybir.dt.int32
+FP8X4 = mybir.dt.float8_e4m3fn_x4
+ALU = mybir.AluOpType
+ACT = mybir.ActivationFunctionType
+
+P = 128
+PACK = 4
+K_PASS = P * PACK
+BANK = 512
+
+TOKENS = 1024
+TOK_TILES = TOKENS // P
+HEADS = 8
+H = 1024
+FF = 3072
+PASSES = H // K_PASS
+CHUNK = 1024
+FF_CHUNKS = FF // CHUNK
+EPS = 1e-7
+
+FLOPS = 2 * TOKENS * H * (H + FF)
+
+
+def tile_disentangledattention_pb_kernel(
+    tc, head_context, h, Wo, bo, ln1_g, ln1_b, Wi, bi, out_0, out_1
+):
+    nc = tc.nc
+    h_rows = h.flatten_outer_dims()
+    a_rows = out_0.flatten_outer_dims()
+    f_rows = out_1.flatten_outer_dims()
+
+    with ExitStack() as ctx:
+        consts = ctx.enter_context(tc.tile_pool(name="consts", bufs=1))
+        keep = ctx.enter_context(tc.tile_pool(name="keep", bufs=1))
+        acts = ctx.enter_context(tc.tile_pool(name="acts", bufs=TOK_TILES))
+        raws = ctx.enter_context(tc.tile_pool(name="raws", bufs=4))
+        stage = ctx.enter_context(tc.tile_pool(name="stage", bufs=2))
+        small = ctx.enter_context(tc.tile_pool(name="small", bufs=2))
+        mid = ctx.enter_context(tc.tile_pool(name="mid", bufs=3))
+        stats = ctx.enter_context(tc.tile_pool(name="stats", bufs=4))
+        fpool = ctx.enter_context(tc.tile_pool(name="fpool", bufs=6))
+        psum_mm = ctx.enter_context(tc.psum_pool(name="psum_mm", bufs=5))
+        psum_tr = ctx.enter_context(tc.psum_pool(name="psum_tr", bufs=3))
+
+        ctx.enter_context(tc.manual_schedule())
+
+        ident_f32 = consts.tile([P, P], F32)
+        make_identity(nc, ident_f32[:])
+        ident_bf16 = consts.tile([P, P], BF16)
+        make_identity(nc, ident_bf16[:])
+        ones_bf16 = consts.tile([P, P], BF16)
+        nc.vector.memset(ones_bf16[:], 1.0)
+        minus_half = consts.tile([P, 1], F32)
+        nc.vector.memset(minus_half[:], -0.5)
+        warm = consts.tile([P, 1], F32)
+        nc.scalar.activation(out=warm[:], in_=minus_half[:], func=ACT.Gelu)
+
+        rows = consts.tile([P, 3 * H + FF], BF16)
+        nc.vector.memset(rows[:, 0 : 3 * H].bitcast(I32), 0)
+        nc.vector.memset(rows[:, 3 * H : 3 * H + FF].bitcast(I32), 0)
+        first = 0
+        for vec in (bo, ln1_g, ln1_b, bi):
+            width = vec.shape[0]
+            nc.scalar.dma_start(
+                out=rows[0:1, first : first + width],
+                in_=vec.rearrange("(o n) -> o n", o=1),
+            )
+            first += width
+        bo_rows = rows[:, 0:H]
+
+        wo_codes = keep.tile([P, PASSES, H], U32, align_bytes=64)
+        wo_scales = keep.tile([P, PASSES, H], U8, align_bytes=64)
+        wi_codes = keep.tile([P, PASSES, FF], U32, align_bytes=64)
+        wi_scales = keep.tile([P, PASSES, FF], U8, align_bytes=64)
+        c_codes = keep.tile([P, TOK_TILES, PASSES, P], U32, align_bytes=64)
+        c_scales = keep.tile([P, TOK_TILES, PASSES, P], U8, align_bytes=64)
+        a_codes = keep.tile([P, TOK_TILES, PASSES, P], U32, align_bytes=64)
+        a_scales = keep.tile([P, TOK_TILES, PASSES, P], U8, align_bytes=64)
+
+        def load_wo(g):
+            raw = raws.tile([P, PACK, CHUNK], BF16, tag="raw")
+            for u in range(2):
+                k0 = g * K_PASS + u * 2 * P
+                nc.sync.dma_start(
+                    out=raw[:, 2 * u : 2 * u + 2, :],
+                    in_=Wo[k0 : k0 + 2 * P, :].rearrange("(q e) c -> q e c", e=2),
+                )
+            return raw
+
+        def load_wi(chunk):
+            j, g = divmod(chunk, PASSES)
+            raw = raws.tile([P, PACK, CHUNK], BF16, tag="raw")
+            nc.sync.dma_start(
+                out=raw[:],
+                in_=Wi[g * K_PASS : (g + 1) * K_PASS, j * CHUNK : (j + 1) * CHUNK].rearrange(
+                    "(t p) c -> p t c", p=P
+                ),
+            )
+            return raw
+
+        def regroup(raw, half):
+            grouped = stage.tile([P, BANK, PACK], BF16, tag="grouped%d" % half, align_bytes=64)
+            dst = grouped[:].rearrange("p (c i) t -> p c t i", i=4)
+            src = raw[:, :, half * BANK : (half + 1) * BANK].rearrange("p t (c i) -> p c t i", i=4)
+            if half == 0:
+                nc.vector.tensor_copy(out=dst, in_=src)
+            else:
+                nc.scalar.copy(out=dst, in_=src)
+            return grouped
+
+        def quantise(grouped, half, codes, scales):
+            cols = slice(half * BANK, (half + 1) * BANK)
+            nc.vector.quantize_mx(
+                out=codes[:, cols].bitcast(FP8X4),
+                scales=scales[:, cols],
+                in_=grouped[:].rearrange("p w t -> p (w t)"),
+            )
+
+        def quantise_wi(grouped, half, chunk):
+            j, g = divmod(chunk, PASSES)
+            cols = slice(j * CHUNK, (j + 1) * CHUNK)
+            quantise(grouped, half, wi_codes[:, g, cols], wi_scales[:, g, cols])
+
+        c_raws = {}
+        h_raws = {}
+        c_groupeds = {}
+        a_groupeds = {}
+        u_tiles = {}
+        a_tiles = {}
+        negmeans = {}
+        rstds = {}
+
+        def load_tokens(i):
+            b = i // (TOK_TILES // 2)
+            s0 = (i % (TOK_TILES // 2)) * P
+            c_raw = acts.tile([P, H], BF16)
+            nc.sync.dma_start(
+                out=c_raw[:].rearrange("s (n d) -> s n d", n=HEADS),
+                in_=head_context[b, :, s0 : s0 + P, :].rearrange("n s d -> s n d"),
+            )
+            c_raws[i] = c_raw
+            h_raw = acts.tile([P, H], BF16)
+            nc.sync.dma_start(out=h_raw[:], in_=h_rows[i * P : (i + 1) * P, :])
+            h_raws[i] = h_raw
+
+        def c_in(i):
+            c_words = c_raws[i][:].bitcast(F32)
+            ct = psum_tr.tile([P, PACK, P], F32, tag="tr")
+            for w in range(PACK):
+                nc.tensor.transpose(ct[:, w, :], c_words[:, w * P : (w + 1) * P], ident_f32[:])
+            c_grouped = small.tile([P, H], BF16, align_bytes=64)
+            nc.scalar.copy(
+                out=c_grouped[:].bitcast(F32).rearrange("q (g r u) -> q g r u", g=PASSES, u=2),
+                in_=ct[:].rearrange("q (g u) r -> q g r u", u=2),
+            )
+            c_groupeds[i] = c_grouped
+
+        def residual_in(i):
+            u = mid.tile([P, H], F32)
+            for n in range(H // BANK):
+                cols = slice(n * BANK, (n + 1) * BANK)
+                hb = psum_mm.tile([P, BANK], F32, tag="mm")
+                nc.tensor.matmul(hb[:], lhsT=ident_bf16[:], rhs=h_raws[i][:, cols], start=True, stop=False)
+                nc.tensor.matmul(hb[:], lhsT=ones_bf16[:], rhs=bo_rows[:, cols], start=False, stop=True)
+                nc.scalar.copy(out=u[:, cols], in_=hb[:])
+            u_tiles[i] = u
+
+        def quantise_c(i):
+            nc.vector.quantize_mx(
+                out=c_codes[:, i].rearrange("q g r -> q (g r)").bitcast(FP8X4),
+                scales=c_scales[:, i].rearrange("q g r -> q (g r)"),
+                in_=c_groupeds[i][:],
+            )
+
+        def project(i):
+            u = u_tiles[i]
+            sums = stats.tile([P, H // BANK], F32)
+            for n in range(H // BANK):
+                cols = slice(n * BANK, (n + 1) * BANK)
+                y = psum_mm.tile([P, BANK], F32, tag="mm")
+                for g in range(PASSES):
+                    nc.tensor.matmul_mx(
+                        out=y[:],
+                        lhsT=c_codes[:, i, g, :].bitcast(FP8X4),
+                        lhsT_scale=c_scales[:, i, g, :],
+                        rhs=wo_codes[:, g, cols].bitcast(FP8X4),
+                        rhs_scale=wo_scales[:, g, cols],
+                        start=(g == 0),
+                        stop=(g == PASSES - 1),
+                    )
+                nc.vector.scalar_tensor_tensor(
+                    out=u[:, cols], in0=y[:], scalar=1.0, in1=u[:, cols],
+                    op0=ALU.mult, op1=ALU.add, accum_out=sums[:, n : n + 1],
+                )
+            negmean = stats.tile([P, 1], F32)
+            nc.vector.tensor_scalar(
+                out=negmean[:], in0=sums[:, 0:1], scalar1=sums[:, 1:2], scalar2=-1.0 / H,
+                op0=ALU.add, op1=ALU.mult,
+            )
+            negmeans[i] = negmean
+
+        def variance(i):
+            squares = small.tile([P, H], BF16)
+            ssq = stats.tile([P, 1], F32)
+            nc.scalar.activation(
+                out=squares[:], in_=u_tiles[i][:], func=ACT.Square, bias=negmeans[i][:, 0:1],
+                accum_out=ssq[:],
+            )
+            var_eps = stats.tile([P, 1], F32)
+            nc.gpsimd.tensor_scalar(
+                out=var_eps[:], in0=ssq[:], scalar1=1.0 / H, scalar2=EPS, op0=ALU.mult, op1=ALU.add,
+            )
+            rstd = stats.tile([P, 1], F32)
+            nc.gpsimd.tensor_tensor(out=rstd[:], in0=var_eps[:], in1=minus_half[:], op=ALU.pow)
+            rstds[i] = rstd
+
+        def centre(i):
+            a_t = mid.tile([P, H], F32)
+            nc.vector.scalar_tensor_tensor(
+                out=a_t[:], in0=u_tiles[i][:], scalar=negmeans[i][:, 0:1], in1=g_bc,
+                op0=ALU.add, op1=ALU.mult,
+            )
+            a_tiles[i] = a_t
+
+        def scale_shift(i):
+            a_t = a_tiles[i]
+            nc.vector.scalar_tensor_tensor(
+                out=a_t[:], in0=a_t[:], scalar=rstds[i][:, 0:1], in1=b_bc, op0=ALU.mult, op1=ALU.add,
+            )
+            nc.sync.dma_start(out=a_rows[i * P : (i + 1) * P, :], in_=a_t[:])
+
+        def a_transposed(i):
+            a_grouped = small.tile([P, PASSES, P, PACK], BF16, align_bytes=64)
+            for g in range(PASSES):
+                at = psum_tr.tile([P, PACK, P], F32, tag="tr")
+                for t in range(PACK):
+                    k0 = g * K_PASS + t * P
+                    nc.tensor.transpose(at[:, t, :], a_tiles[i][:, k0 : k0 + P], ident_f32[:])
+                nc.scalar.copy(out=a_grouped[:, g], in_=at[:].rearrange("p t r -> p r t"))
+            a_groupeds[i] = a_grouped
+
+        def quantise_a(i):
+            nc.vector.quantize_mx(
+                out=a_codes[:, i].rearrange("p g r -> p (g r)").bitcast(FP8X4),
+                scales=a_scales[:, i].rearrange("p g r -> p (g r)"),
+                in_=a_groupeds[i][:].rearrange("p g r t -> p (g r t)"),
+            )
+
+        def back_sums(i, j):
+            f_t = fpool.tile([P, CHUNK], F32)
+            for n in range(CHUNK // BANK):
+                cols = slice(j * CHUNK + n * BANK, j * CHUNK + (n + 1) * BANK)
+                acc = psum_mm.tile([P, BANK], F32, tag="mm")
+                for g in range(PASSES):
+                    nc.tensor.matmul_mx(
+                        out=acc[:],
+                        lhsT=a_codes[:, i, g, :].bitcast(FP8X4),
+                        lhsT_scale=a_scales[:, i, g, :],
+                        rhs=wi_codes[:, g, cols].bitcast(FP8X4),
+                        rhs_scale=wi_scales[:, g, cols],
+                        start=(g == 0),
+                        stop=(g == PASSES - 1),
+                    )
+                nc.vector.tensor_tensor(
+                    out=f_t[:, n * BANK : (n + 1) * BANK], in0=acc[:], in1=bi_bc[:, cols], op=ALU.add,
+                )
+            return f_t
+
+        def back_gelu(i, j, f_t):
+            nc.scalar.activation(out=f_t[:], in_=f_t[:], func=ACT.Gelu)
+            nc.sync.dma_start(
+                out=f_rows[i * P : (i + 1) * P, j * CHUNK : (j + 1) * CHUNK], in_=f_t[:]
+            )
+
+        def broadcast(m):
+            bc = psum_tr.tile([P, 2 * BANK], BF16, tag="tr")
+            for n in range(2):
+                nc.tensor.matmul(
+                    bc[:, n * BANK : (n + 1) * BANK],
+                    lhsT=ones_bf16[:],
+                    rhs=rows[:, H + (2 * m + n) * BANK : H + (2 * m + n + 1) * BANK],
+                    start=True,
+                    stop=True,
+                )
+            nc.scalar.copy(out=row_bc[:, 2 * m * BANK : 2 * (m + 1) * BANK], in_=bc[:])
+
+        row_bc = consts.tile([P, 2 * H + FF], BF16)
+        g_bc = row_bc[:, 0:H]
+        b_bc = row_bc[:, H : 2 * H]
+        bi_bc = row_bc[:, 2 * H : 2 * H + FF]
+
+        wo_raws = {}
+        wi_raws = {}
+        for g in range(PASSES):
+            wo_raws[g] = load_wo(g)
+        load_tokens(0)
+        load_tokens(1)
+        for chunk in range(2):
+            wi_raws[chunk] = load_wi(chunk)
+        load_tokens(2)
+
+        wo_grouped = {}
+        for g in range(PASSES):
+            for half in range(2):
+                wo_grouped[g, half] = regroup(wo_raws[g], half)
+            wi_raws[2 + g] = load_wi(2 + g)
+            if g == 0:
+                quantise(wo_grouped[0, 0], 0, wo_codes[:, 0, :], wo_scales[:, 0, :])
+        load_tokens(3)
+        quantise(wo_grouped[0, 1], 1, wo_codes[:, 0, :], wo_scales[:, 0, :])
+        quantise(wo_grouped[1, 0], 0, wo_codes[:, 1, :], wo_scales[:, 1, :])
+        c_in(0)
+        residual_in(0)
+        quantise(wo_grouped[1, 1], 1, wo_codes[:, 1, :], wo_scales[:, 1, :])
+        quantise_c(0)
+        broadcast(0)
+        broadcast(1)
+
+        for r in range(TOK_TILES + 2):
+            comes_in = r + 1 < TOK_TILES
+            projects = r < TOK_TILES
+            normalises = 0 <= r - 1 < TOK_TILES
+            goes_out = r - 2 >= 0
+            chunk = 3 * r
+
+            if not goes_out:
+                by_scalar = regroup(wi_raws[chunk], 1)
+            if normalises:
+                scale_shift(r - 1)
+            if projects:
+                project(r)
+            if comes_in:
+                c_in(r + 1)
+                residual_in(r + 1)
+            if projects:
+                variance(r)
+                centre(r)
+            if goes_out:
+                f_0 = back_sums(r - 2, 0)
+            if normalises:
+                a_transposed(r - 1)
+            if goes_out:
+                back_gelu(r - 2, 0, f_0)
+                f_1 = back_sums(r - 2, 1)
+                back_gelu(r - 2, 1, f_1)
+            else:
+                by_vector = regroup(wi_raws[chunk], 0)
+                if chunk + 4 < FF_CHUNKS * PASSES:
+                    wi_raws[chunk + 4] = load_wi(chunk + 4)
+                quantise_wi(by_scalar, 1, chunk)
+                quantise_wi(by_vector, 0, chunk)
+            if normalises:
+                quantise_a(r - 1)
+            if comes_in:
+                quantise_c(r + 1)
+            if goes_out:
+                f_2 = back_sums(r - 2, 2)
+                back_gelu(r - 2, 2, f_2)
+            else:
+                for chunk in (3 * r + 1, 3 * r + 2):
+                    by_scalar = regroup(wi_raws[chunk], 1)
+                    by_vector = regroup(wi_raws[chunk], 0)
+                    if chunk + 4 < FF_CHUNKS * PASSES:
+                        wi_raws[chunk + 4] = load_wi(chunk + 4)
+                    quantise_wi(by_vector, 0, chunk)
+                    quantise_wi(by_scalar, 1, chunk)
+            if r == 0:
+                for i in range(4, TOK_TILES):
+                    load_tokens(i)
+            if r == 1:
+                for m in range(2, (2 * H + FF) // (2 * BANK)):
+                    broadcast(m)

@@ -225,10 +225,13 @@ def tile_disentangledattention_pb_kernel(
 
         def centre(i):
             a_t = mid.tile([P, H], F32)
-            nc.vector.scalar_tensor_tensor(
-                out=a_t[:], in0=u_tiles[i][:], scalar=negmeans[i][:, 0:1], in1=g_bc,
-                op0=ALU.add, op1=ALU.mult,
-            )
+            for n in range(H // BANK):
+                cols = slice(n * BANK, (n + 1) * BANK)
+                nc.gpsimd.tensor_scalar(
+                    out=a_t[:, cols], in0=u_tiles[i][:, cols], scalar1=negmeans[i][:, 0:1], scalar2=1.0,
+                    op0=ALU.add, op1=ALU.mult,
+                )
+                nc.gpsimd.tensor_tensor(out=a_t[:, cols], in0=a_t[:, cols], in1=g_bc[:, cols], op=ALU.mult)
             a_tiles[i] = a_t
 
         def scale_shift(i):
@@ -338,12 +341,12 @@ def tile_disentangledattention_pb_kernel(
                 scale_shift(r - 1)
             if projects:
                 project(r)
+                centre(r)
             if comes_in:
                 c_in(r + 1)
                 residual_in(r + 1)
             if projects:
                 variance(r)
-                centre(r)
             if goes_out:
                 f_0 = back_sums(r - 2, 0)
             if normalises:

@@ -51,8 +51,6 @@ def tile_disentangledattention_pb_kernel(
         psum_mm = ctx.enter_context(tc.psum_pool(name="psum_mm", bufs=5))
         psum_tr = ctx.enter_context(tc.psum_pool(name="psum_tr", bufs=3))
 
-        ctx.enter_context(tc.manual_schedule())
-
         ident_f32 = consts.tile([P, P], F32)
         make_identity(nc, ident_f32[:])
         ident_bf16 = consts.tile([P, P], BF16)
@@ -225,13 +223,10 @@ def tile_disentangledattention_pb_kernel(
 
         def centre(i):
             a_t = mid.tile([P, H], F32)
-            for n in range(H // BANK):
-                cols = slice(n * BANK, (n + 1) * BANK)
-                nc.gpsimd.tensor_scalar(
-                    out=a_t[:, cols], in0=u_tiles[i][:, cols], scalar1=negmeans[i][:, 0:1], scalar2=1.0,
-                    op0=ALU.add, op1=ALU.mult,
-                )
-                nc.gpsimd.tensor_tensor(out=a_t[:, cols], in0=a_t[:, cols], in1=g_bc[:, cols], op=ALU.mult)
+            nc.vector.scalar_tensor_tensor(
+                out=a_t[:], in0=u_tiles[i][:], scalar=negmeans[i][:, 0:1], in1=g_bc,
+                op0=ALU.add, op1=ALU.mult,
+            )
             a_tiles[i] = a_t
 
         def scale_shift(i):
@@ -258,10 +253,10 @@ def tile_disentangledattention_pb_kernel(
                 in_=a_groupeds[i][:].rearrange("p g r t -> p (g r t)"),
             )
 
-        def back_sums(i, j):
+        def back_sums(i, first, width):
             f_t = fpool.tile([P, CHUNK], F32)
-            for n in range(CHUNK // BANK):
-                cols = slice(j * CHUNK + n * BANK, j * CHUNK + (n + 1) * BANK)
+            for n in range(width // BANK):
+                cols = slice(first + n * BANK, first + (n + 1) * BANK)
                 acc = psum_mm.tile([P, BANK], F32, tag="mm")
                 for g in range(PASSES):
                     nc.tensor.matmul_mx(
@@ -278,10 +273,10 @@ def tile_disentangledattention_pb_kernel(
                 )
             return f_t
 
-        def back_gelu(i, j, f_t):
-            nc.scalar.activation(out=f_t[:], in_=f_t[:], func=ACT.Gelu)
+        def back_gelu(i, first, width, f_t):
+            nc.scalar.activation(out=f_t[:, 0:width], in_=f_t[:, 0:width], func=ACT.Gelu)
             nc.sync.dma_start(
-                out=f_rows[i * P : (i + 1) * P, j * CHUNK : (j + 1) * CHUNK], in_=f_t[:]
+                out=f_rows[i * P : (i + 1) * P, first : first + width], in_=f_t[:, 0:width]
             )
 
         def broadcast(m):
@@ -341,20 +336,20 @@ def tile_disentangledattention_pb_kernel(
                 scale_shift(r - 1)
             if projects:
                 project(r)
-                centre(r)
             if comes_in:
                 c_in(r + 1)
                 residual_in(r + 1)
             if projects:
                 variance(r)
+                centre(r)
             if goes_out:
-                f_0 = back_sums(r - 2, 0)
+                f_0 = back_sums(r - 2, 0, CHUNK)
             if normalises:
                 a_transposed(r - 1)
             if goes_out:
-                back_gelu(r - 2, 0, f_0)
-                f_1 = back_sums(r - 2, 1)
-                back_gelu(r - 2, 1, f_1)
+                back_gelu(r - 2, 0, CHUNK, f_0)
+                f_1 = back_sums(r - 2, CHUNK, CHUNK)
+                back_gelu(r - 2, CHUNK, CHUNK, f_1)
             else:
                 by_vector = regroup(wi_raws[chunk], 0)
                 if chunk + 4 < FF_CHUNKS * PASSES:
@@ -366,8 +361,10 @@ def tile_disentangledattention_pb_kernel(
             if comes_in:
                 quantise_c(r + 1)
             if goes_out:
-                f_2 = back_sums(r - 2, 2)
-                back_gelu(r - 2, 2, f_2)
+                width = BANK if r - 2 == TOK_TILES - 1 else CHUNK
+                for first in range(2 * CHUNK, FF, width):
+                    f_2 = back_sums(r - 2, first, width)
+                    back_gelu(r - 2, first, width, f_2)
             else:
                 for chunk in (3 * r + 1, 3 * r + 2):
                     by_scalar = regroup(wi_raws[chunk], 1)

@@ -27,6 +27,11 @@ CHUNK = 1024
 FF_CHUNKS = FF // CHUNK
 EPS = 1e-7
 
+GPSIMD_FROM = 6
+PIECE = 64
+FIRST_ROUND = (2, 3, 5)
+GELU_DELAY = 4
+
 FLOPS = 2 * TOKENS * H * (H + FF)
 
 
@@ -48,8 +53,9 @@ def tile_disentangledattention_pb_kernel(
         mid = ctx.enter_context(tc.tile_pool(name="mid", bufs=3))
         stats = ctx.enter_context(tc.tile_pool(name="stats", bufs=4))
         fpool = ctx.enter_context(tc.tile_pool(name="fpool", bufs=6))
-        psum_mm = ctx.enter_context(tc.psum_pool(name="psum_mm", bufs=5))
-        psum_tr = ctx.enter_context(tc.psum_pool(name="psum_tr", bufs=3))
+        psum_mm = ctx.enter_context(tc.psum_pool(name="psum_mm", bufs=4))
+        psum_tr = ctx.enter_context(tc.psum_pool(name="psum_tr", bufs=2))
+        psum_rows = ctx.enter_context(tc.psum_pool(name="psum_rows", bufs=1))
 
         ident_f32 = consts.tile([P, P], F32)
         make_identity(nc, ident_f32[:])
@@ -105,14 +111,22 @@ def tile_disentangledattention_pb_kernel(
             )
             return raw
 
-        def regroup(raw, half):
-            grouped = stage.tile([P, BANK, PACK], BF16, tag="grouped%d" % half, align_bytes=64)
-            dst = grouped[:].rearrange("p (c i) t -> p c t i", i=4)
-            src = raw[:, :, half * BANK : (half + 1) * BANK].rearrange("p t (c i) -> p c t i", i=4)
-            if half == 0:
-                nc.vector.tensor_copy(out=dst, in_=src)
-            else:
-                nc.scalar.copy(out=dst, in_=src)
+        def regroup(raw, half, on_gpsimd=False):
+            tag = "grouped_g" if on_gpsimd else "grouped%d" % half
+            grouped = stage.tile([P, BANK, PACK], BF16, tag=tag, align_bytes=64)
+            raw_half = raw[:, :, half * BANK : (half + 1) * BANK]
+            width = PIECE if on_gpsimd else BANK
+            for c0 in range(0, BANK, width):
+                dst = grouped[:, c0 : c0 + width, :].rearrange("p (c i) t -> p c t i", i=4)
+                src = raw_half[:, :, c0 : c0 + width].rearrange("p t (c i) -> p c t i", i=4)
+                if on_gpsimd:
+                    nc.gpsimd.tensor_scalar(
+                        out=dst, in0=src, scalar1=1.0, scalar2=0.0, op0=ALU.mult, op1=ALU.add
+                    )
+                elif half == 0:
+                    nc.vector.tensor_copy(out=dst, in_=src)
+                else:
+                    nc.scalar.copy(out=dst, in_=src)
             return grouped
 
         def quantise(grouped, half, codes, scales):
@@ -224,7 +238,7 @@ def tile_disentangledattention_pb_kernel(
         def centre(i):
             a_t = mid.tile([P, H], F32)
             nc.vector.scalar_tensor_tensor(
-                out=a_t[:], in0=u_tiles[i][:], scalar=negmeans[i][:, 0:1], in1=g_bc,
+                out=a_t[:], in0=u_tiles[i][:], scalar=negmeans[i][:, 0:1], in1=g_psum[:],
                 op0=ALU.add, op1=ALU.mult,
             )
             a_tiles[i] = a_t
@@ -232,7 +246,7 @@ def tile_disentangledattention_pb_kernel(
         def scale_shift(i):
             a_t = a_tiles[i]
             nc.vector.scalar_tensor_tensor(
-                out=a_t[:], in0=a_t[:], scalar=rstds[i][:, 0:1], in1=b_bc, op0=ALU.mult, op1=ALU.add,
+                out=a_t[:], in0=a_t[:], scalar=rstds[i][:, 0:1], in1=b_psum[:], op0=ALU.mult, op1=ALU.add,
             )
             nc.sync.dma_start(out=a_rows[i * P : (i + 1) * P, :], in_=a_t[:])
 
@@ -273,28 +287,40 @@ def tile_disentangledattention_pb_kernel(
                 )
             return f_t
 
-        def back_gelu(i, first, width, f_t):
+        sums_out = []
+        gelus_out = []
+
+        def back(i, first, width):
+            sums_out.append((i, first, width, back_sums(i, first, width)))
+            if len(sums_out) - len(gelus_out) > GELU_DELAY:
+                gelu(*sums_out[len(gelus_out)])
+
+        def gelu(i, first, width, f_t):
+            gelus_out.append(i)
             nc.scalar.activation(out=f_t[:, 0:width], in_=f_t[:, 0:width], func=ACT.Gelu)
             nc.sync.dma_start(
                 out=f_rows[i * P : (i + 1) * P, first : first + width], in_=f_t[:, 0:width]
             )
 
-        def broadcast(m):
-            bc = psum_tr.tile([P, 2 * BANK], BF16, tag="tr")
+        def spread(bank, first):
             for n in range(2):
+                cols = slice(first + n * BANK, first + (n + 1) * BANK)
                 nc.tensor.matmul(
-                    bc[:, n * BANK : (n + 1) * BANK],
+                    bank[:, n * BANK : (n + 1) * BANK],
                     lhsT=ones_bf16[:],
-                    rhs=rows[:, H + (2 * m + n) * BANK : H + (2 * m + n + 1) * BANK],
+                    rhs=rows[:, cols],
                     start=True,
                     stop=True,
                 )
-            nc.scalar.copy(out=row_bc[:, 2 * m * BANK : 2 * (m + 1) * BANK], in_=bc[:])
 
-        row_bc = consts.tile([P, 2 * H + FF], BF16)
-        g_bc = row_bc[:, 0:H]
-        b_bc = row_bc[:, H : 2 * H]
-        bi_bc = row_bc[:, 2 * H : 2 * H + FF]
+        def spread_bi(j):
+            bank = psum_tr.tile([P, 2 * BANK], BF16, tag="tr")
+            spread(bank, 3 * H + j * CHUNK)
+            nc.scalar.copy(out=bi_bc[:, j * CHUNK : (j + 1) * CHUNK], in_=bank[:])
+
+        bi_bc = consts.tile([P, FF], BF16)
+        g_psum = psum_rows.tile([P, H], BF16)
+        b_psum = psum_rows.tile([P, H], BF16)
 
         wo_raws = {}
         wi_raws = {}
@@ -320,18 +346,36 @@ def tile_disentangledattention_pb_kernel(
         residual_in(0)
         quantise(wo_grouped[1, 1], 1, wo_codes[:, 1, :], wo_scales[:, 1, :])
         quantise_c(0)
-        broadcast(0)
-        broadcast(1)
+        spread(g_psum, H)
+        spread(b_psum, 2 * H)
+
+        def prepare(chunk):
+            raw = wi_raws[chunk]
+            half_1 = regroup(raw, 1)
+            half_0 = regroup(raw, 0, on_gpsimd=chunk >= GPSIMD_FROM)
+            if chunk + 4 < FF_CHUNKS * PASSES:
+                wi_raws[chunk + 4] = load_wi(chunk + 4)
+            return half_0, half_1
+
+        def quantise_chunk(chunk, halves):
+            for half in range(2):
+                quantise_wi(halves[half], half, chunk)
+
+        pieces = {}
+        for j in range(FF_CHUNKS):
+            for d in range(TOK_TILES):
+                pieces.setdefault(max(d + 2, FIRST_ROUND[j] + (d + 1) // 2), []).append((d, j))
+        chunks = {0: [0, 1], 1: [2], 2: [3], 3: [4], 4: [5]}
 
         for r in range(TOK_TILES + 2):
             comes_in = r + 1 < TOK_TILES
             projects = r < TOK_TILES
             normalises = 0 <= r - 1 < TOK_TILES
-            goes_out = r - 2 >= 0
-            chunk = 3 * r
+            going_out = pieces.get(r, [])
+            new_chunks = chunks.get(r, [])
 
-            if not goes_out:
-                by_scalar = regroup(wi_raws[chunk], 1)
+            for chunk in new_chunks[0:1]:
+                halves = prepare(chunk)
             if normalises:
                 scale_shift(r - 1)
             if projects:
@@ -342,40 +386,29 @@ def tile_disentangledattention_pb_kernel(
             if projects:
                 variance(r)
                 centre(r)
-            if goes_out:
-                f_0 = back_sums(r - 2, 0, CHUNK)
+            for d, j in going_out[0:1]:
+                back(d, j * CHUNK, CHUNK)
             if normalises:
                 a_transposed(r - 1)
-            if goes_out:
-                back_gelu(r - 2, 0, CHUNK, f_0)
-                f_1 = back_sums(r - 2, CHUNK, CHUNK)
-                back_gelu(r - 2, CHUNK, CHUNK, f_1)
-            else:
-                by_vector = regroup(wi_raws[chunk], 0)
-                if chunk + 4 < FF_CHUNKS * PASSES:
-                    wi_raws[chunk + 4] = load_wi(chunk + 4)
-                quantise_wi(by_scalar, 1, chunk)
-                quantise_wi(by_vector, 0, chunk)
+            for d, j in going_out[1:2]:
+                back(d, j * CHUNK, CHUNK)
+            for chunk in new_chunks[0:1]:
+                quantise_chunk(chunk, halves)
             if normalises:
                 quantise_a(r - 1)
             if comes_in:
                 quantise_c(r + 1)
-            if goes_out:
-                width = BANK if r - 2 == TOK_TILES - 1 else CHUNK
-                for first in range(2 * CHUNK, FF, width):
-                    f_2 = back_sums(r - 2, first, width)
-                    back_gelu(r - 2, first, width, f_2)
-            else:
-                for chunk in (3 * r + 1, 3 * r + 2):
-                    by_scalar = regroup(wi_raws[chunk], 1)
-                    by_vector = regroup(wi_raws[chunk], 0)
-                    if chunk + 4 < FF_CHUNKS * PASSES:
-                        wi_raws[chunk + 4] = load_wi(chunk + 4)
-                    quantise_wi(by_vector, 0, chunk)
-                    quantise_wi(by_scalar, 1, chunk)
+            for d, j in going_out[2:]:
+                width = BANK if (d, j) == (TOK_TILES - 1, FF_CHUNKS - 1) else CHUNK
+                for first in range(j * CHUNK, (j + 1) * CHUNK, width):
+                    back(d, first, width)
+            for chunk in new_chunks[1:]:
+                quantise_chunk(chunk, prepare(chunk))
             if r == 0:
                 for i in range(4, TOK_TILES):
                     load_tokens(i)
             if r == 1:
-                for m in range(2, (2 * H + FF) // (2 * BANK)):
-                    broadcast(m)
+                for j in range(FF_CHUNKS):
+                    spread_bi(j)
+        for piece in sums_out[len(gelus_out) :]:
+            gelu(*piece)

@@ -117,8 +117,8 @@ def tile_disentangledattention_pb_kernel(
             raw_half = raw[:, :, half * BANK : (half + 1) * BANK]
             width = PIECE if on_gpsimd else BANK
             for c0 in range(0, BANK, width):
-                dst = grouped[:, c0 : c0 + width, :].rearrange("p (c i) t -> p c t i", i=4)
-                src = raw_half[:, :, c0 : c0 + width].rearrange("p t (c i) -> p c t i", i=4)
+                dst = grouped[:, c0 : c0 + width, :].rearrange("p (c i) t -> p c t i", i=8)
+                src = raw_half[:, :, c0 : c0 + width].rearrange("p t (c i) -> p c t i", i=8)
                 if on_gpsimd:
                     nc.gpsimd.tensor_scalar(
                         out=dst, in0=src, scalar1=1.0, scalar2=0.0, op0=ALU.mult, op1=ALU.add

@@ -26,9 +26,9 @@ PASSES = H // K_PASS
 CHUNK = 1024
 FF_CHUNKS = FF // CHUNK
 EPS = 1e-7
+HV = (256, 256)
+G1V = (512, 0)
 
-GPSIMD_FROM = 6
-PIECE = 64
 FIRST_ROUND = (2, 3, 5)
 GELU_DELAY = 4
 
@@ -92,11 +92,18 @@ def tile_disentangledattention_pb_kernel(
 
         def load_wo(g):
             raw = raws.tile([P, PACK, CHUNK], BF16, tag="raw")
-            for u in range(2):
-                k0 = g * K_PASS + u * 2 * P
+            if g == 0:
+                for c0 in range(0, CHUNK, BANK):
+                    for u in range(2):
+                        k0 = u * 2 * P
+                        nc.sync.dma_start(
+                            out=raw[:, 2 * u : 2 * u + 2, c0 : c0 + BANK],
+                            in_=Wo[k0 : k0 + 2 * P, c0 : c0 + BANK].rearrange("(q e) c -> q e c", e=2),
+                        )
+            else:
                 nc.sync.dma_start(
-                    out=raw[:, 2 * u : 2 * u + 2, :],
-                    in_=Wo[k0 : k0 + 2 * P, :].rearrange("(q e) c -> q e c", e=2),
+                    out=raw[:].rearrange("q (u e) c -> q u (e c)", u=2),
+                    in_=Wo[g * K_PASS : (g + 1) * K_PASS, :].rearrange("(u q e) c -> q u (e c)", u=2, e=2),
                 )
             return raw
 
@@ -111,22 +118,18 @@ def tile_disentangledattention_pb_kernel(
             )
             return raw
 
-        def regroup(raw, half, on_gpsimd=False):
-            tag = "grouped_g" if on_gpsimd else "grouped%d" % half
-            grouped = stage.tile([P, BANK, PACK], BF16, tag=tag, align_bytes=64)
+        def regroup(raw, half, by_vector):
+            grouped = stage.tile([P, BANK, PACK], BF16, tag="grouped%d" % half, align_bytes=64)
             raw_half = raw[:, :, half * BANK : (half + 1) * BANK]
-            width = PIECE if on_gpsimd else BANK
-            for c0 in range(0, BANK, width):
-                dst = grouped[:, c0 : c0 + width, :].rearrange("p (c i) t -> p c t i", i=8)
-                src = raw_half[:, :, c0 : c0 + width].rearrange("p t (c i) -> p c t i", i=8)
-                if on_gpsimd:
-                    nc.gpsimd.tensor_scalar(
-                        out=dst, in0=src, scalar1=1.0, scalar2=0.0, op0=ALU.mult, op1=ALU.add
+            for copy, c0, c1 in (
+                (nc.vector.tensor_copy, 0, by_vector),
+                (nc.scalar.copy, by_vector, BANK),
+            ):
+                if c0 < c1:
+                    copy(
+                        out=grouped[:, c0:c1, :].rearrange("p (c i) t -> p c t i", i=8),
+                        in_=raw_half[:, :, c0:c1].rearrange("p t (c i) -> p c t i", i=8),
                     )
-                elif half == 0:
-                    nc.vector.tensor_copy(out=dst, in_=src)
-                else:
-                    nc.scalar.copy(out=dst, in_=src)
             return grouped
 
         def quantise(grouped, half, codes, scales):
@@ -327,18 +330,19 @@ def tile_disentangledattention_pb_kernel(
         for g in range(PASSES):
             wo_raws[g] = load_wo(g)
         load_tokens(0)
+        wi_raws[0] = load_wi(0)
         load_tokens(1)
-        for chunk in range(2):
-            wi_raws[chunk] = load_wi(chunk)
+        wi_raws[1] = load_wi(1)
         load_tokens(2)
 
         wo_grouped = {}
-        for g in range(PASSES):
-            for half in range(2):
-                wo_grouped[g, half] = regroup(wo_raws[g], half)
-            wi_raws[2 + g] = load_wi(2 + g)
-            if g == 0:
-                quantise(wo_grouped[0, 0], 0, wo_codes[:, 0, :], wo_scales[:, 0, :])
+        for half in range(2):
+            wo_grouped[0, half] = regroup(wo_raws[0], half, HV[half])
+        wi_raws[2] = load_wi(2)
+        quantise(wo_grouped[0, 0], 0, wo_codes[:, 0, :], wo_scales[:, 0, :])
+        for half in range(2):
+            wo_grouped[1, half] = regroup(wo_raws[1], half, G1V[half])
+        wi_raws[3] = load_wi(3)
         load_tokens(3)
         quantise(wo_grouped[0, 1], 1, wo_codes[:, 0, :], wo_scales[:, 0, :])
         quantise(wo_grouped[1, 0], 0, wo_codes[:, 1, :], wo_scales[:, 1, :])
@@ -351,8 +355,8 @@ def tile_disentangledattention_pb_kernel(
 
         def prepare(chunk):
             raw = wi_raws[chunk]
-            half_1 = regroup(raw, 1)
-            half_0 = regroup(raw, 0, on_gpsimd=chunk >= GPSIMD_FROM)
+            half_1 = regroup(raw, 1, 0)
+            half_0 = regroup(raw, 0, BANK)
             if chunk + 4 < FF_CHUNKS * PASSES:
                 wi_raws[chunk + 4] = load_wi(chunk + 4)
             return half_0, half_1
@@ -381,8 +385,8 @@ def tile_disentangledattention_pb_kernel(
             if projects:
                 project(r)
             if comes_in:
-                c_in(r + 1)
                 residual_in(r + 1)
+                c_in(r + 1)
             if projects:
                 variance(r)
                 centre(r)

@@ -46,13 +46,14 @@ def tile_disentangledattention_pb_kernel(
     with ExitStack() as ctx:
         consts = ctx.enter_context(tc.tile_pool(name="consts", bufs=1))
         keep = ctx.enter_context(tc.tile_pool(name="keep", bufs=1))
-        acts = ctx.enter_context(tc.tile_pool(name="acts", bufs=TOK_TILES))
+        acts = ctx.enter_context(tc.tile_pool(name="acts", bufs=6))
         raws = ctx.enter_context(tc.tile_pool(name="raws", bufs=4))
         stage = ctx.enter_context(tc.tile_pool(name="stage", bufs=2))
         small = ctx.enter_context(tc.tile_pool(name="small", bufs=2))
         mid = ctx.enter_context(tc.tile_pool(name="mid", bufs=3))
         stats = ctx.enter_context(tc.tile_pool(name="stats", bufs=4))
-        fpool = ctx.enter_context(tc.tile_pool(name="fpool", bufs=6))
+        fpool = ctx.enter_context(tc.tile_pool(name="fpool", bufs=5))
+        outs = ctx.enter_context(tc.tile_pool(name="outs", bufs=6))
         psum_mm = ctx.enter_context(tc.psum_pool(name="psum_mm", bufs=4))
         psum_tr = ctx.enter_context(tc.psum_pool(name="psum_tr", bufs=2))
         psum_rows = ctx.enter_context(tc.psum_pool(name="psum_rows", bufs=1))
@@ -300,9 +301,10 @@ def tile_disentangledattention_pb_kernel(
 
         def gelu(i, first, width, f_t):
             gelus_out.append(i)
-            nc.scalar.activation(out=f_t[:, 0:width], in_=f_t[:, 0:width], func=ACT.Gelu)
+            f_out = outs.tile([P, CHUNK], F32)
+            nc.scalar.activation(out=f_out[:, 0:width], in_=f_t[:, 0:width], func=ACT.Gelu)
             nc.sync.dma_start(
-                out=f_rows[i * P : (i + 1) * P, first : first + width], in_=f_t[:, 0:width]
+                out=f_rows[i * P : (i + 1) * P, first : first + width], in_=f_out[:, 0:width]
             )
 
         def spread(bank, first):

@@ -46,8 +46,8 @@ def tile_disentangledattention_pb_kernel(
     with ExitStack() as ctx:
         consts = ctx.enter_context(tc.tile_pool(name="consts", bufs=1))
         keep = ctx.enter_context(tc.tile_pool(name="keep", bufs=1))
-        acts = ctx.enter_context(tc.tile_pool(name="acts", bufs=6))
-        raws = ctx.enter_context(tc.tile_pool(name="raws", bufs=4))
+        acts = ctx.enter_context(tc.tile_pool(name="acts", bufs=5))
+        raws = ctx.enter_context(tc.tile_pool(name="raws", bufs=5))
         stage = ctx.enter_context(tc.tile_pool(name="stage", bufs=2))
         small = ctx.enter_context(tc.tile_pool(name="small", bufs=2))
         mid = ctx.enter_context(tc.tile_pool(name="mid", bufs=3))
@@ -69,11 +69,10 @@ def tile_disentangledattention_pb_kernel(
         warm = consts.tile([P, 1], F32)
         nc.scalar.activation(out=warm[:], in_=minus_half[:], func=ACT.Gelu)
 
-        rows = consts.tile([P, 3 * H + FF], BF16)
-        nc.vector.memset(rows[:, 0 : 3 * H].bitcast(I32), 0)
-        nc.vector.memset(rows[:, 3 * H : 3 * H + FF].bitcast(I32), 0)
+        rows = consts.tile([P, 3 * H], BF16)
+        nc.vector.memset(rows[:].bitcast(I32), 0)
         first = 0
-        for vec in (bo, ln1_g, ln1_b, bi):
+        for vec in (bo, ln1_g, ln1_b):
             width = vec.shape[0]
             nc.scalar.dma_start(
                 out=rows[0:1, first : first + width],
@@ -81,6 +80,7 @@ def tile_disentangledattention_pb_kernel(
             )
             first += width
         bo_rows = rows[:, 0:H]
+        bi_bc = consts.tile([P, FF], BF16)
 
         wo_codes = keep.tile([P, PASSES, H], U32, align_bytes=64)
         wo_scales = keep.tile([P, PASSES, H], U8, align_bytes=64)
@@ -318,12 +318,6 @@ def tile_disentangledattention_pb_kernel(
                     stop=True,
                 )
 
-        def spread_bi(j):
-            bank = psum_tr.tile([P, 2 * BANK], BF16, tag="tr")
-            spread(bank, 3 * H + j * CHUNK)
-            nc.scalar.copy(out=bi_bc[:, j * CHUNK : (j + 1) * CHUNK], in_=bank[:])
-
-        bi_bc = consts.tile([P, FF], BF16)
         g_psum = psum_rows.tile([P, H], BF16)
         b_psum = psum_rows.tile([P, H], BF16)
 
@@ -331,25 +325,26 @@ def tile_disentangledattention_pb_kernel(
         wi_raws = {}
         for g in range(PASSES):
             wo_raws[g] = load_wo(g)
-        load_tokens(0)
-        wi_raws[0] = load_wi(0)
-        load_tokens(1)
-        wi_raws[1] = load_wi(1)
-        load_tokens(2)
+        for i in range(3):
+            load_tokens(i)
+            wi_raws[i] = load_wi(i)
 
         wo_grouped = {}
         for half in range(2):
             wo_grouped[0, half] = regroup(wo_raws[0], half, HV[half])
-        wi_raws[2] = load_wi(2)
+        load_tokens(3)
+        wi_raws[3] = load_wi(3)
+        nc.sync.dma_start(out=bi_bc[:], in_=bi.partition_broadcast(P))
         quantise(wo_grouped[0, 0], 0, wo_codes[:, 0, :], wo_scales[:, 0, :])
         for half in range(2):
             wo_grouped[1, half] = regroup(wo_raws[1], half, G1V[half])
-        wi_raws[3] = load_wi(3)
-        load_tokens(3)
+        wi_raws[4] = load_wi(4)
+        load_tokens(4)
         quantise(wo_grouped[0, 1], 1, wo_codes[:, 0, :], wo_scales[:, 0, :])
         quantise(wo_grouped[1, 0], 0, wo_codes[:, 1, :], wo_scales[:, 1, :])
         c_in(0)
         residual_in(0)
+        load_tokens(5)
         quantise(wo_grouped[1, 1], 1, wo_codes[:, 1, :], wo_scales[:, 1, :])
         quantise_c(0)
         spread(g_psum, H)
@@ -358,9 +353,9 @@ def tile_disentangledattention_pb_kernel(
         def prepare(chunk):
             raw = wi_raws[chunk]
             half_1 = regroup(raw, 1, 0)
-            half_0 = regroup(raw, 0, BANK)
-            if chunk + 4 < FF_CHUNKS * PASSES:
-                wi_raws[chunk + 4] = load_wi(chunk + 4)
+            half_0 = regroup(raw, 0, BANK - P if chunk >= 3 else BANK)
+            if chunk == 0:
+                wi_raws[5] = load_wi(5)
             return half_0, half_1
 
         def quantise_chunk(chunk, halves):
@@ -389,6 +384,8 @@ def tile_disentangledattention_pb_kernel(
             if comes_in:
                 residual_in(r + 1)
                 c_in(r + 1)
+                if r + 6 < TOK_TILES:
+                    load_tokens(r + 6)
             if projects:
                 variance(r)
                 centre(r)
@@ -410,11 +407,5 @@ def tile_disentangledattention_pb_kernel(
                     back(d, first, width)
             for chunk in new_chunks[1:]:
                 quantise_chunk(chunk, prepare(chunk))
-            if r == 0:
-                for i in range(4, TOK_TILES):
-                    load_tokens(i)
-            if r == 1:
-                for j in range(FF_CHUNKS):
-                    spread_bi(j)
         for piece in sums_out[len(gelus_out) :]:
             gelu(*piece)

from contextlib import ExitStack

import concourse.mybir as mybir
from concourse.masks import make_identity

F32 = mybir.dt.float32
BF16 = mybir.dt.bfloat16
U32 = mybir.dt.uint32
U8 = mybir.dt.uint8
I32 = mybir.dt.int32
FP8X4 = mybir.dt.float8_e4m3fn_x4
ALU = mybir.AluOpType
ACT = mybir.ActivationFunctionType

P = 128
PACK = 4
K_PASS = P * PACK
BANK = 512

TOKENS = 1024
TOK_TILES = TOKENS // P
HEADS = 8
H = 1024
FF = 3072
PASSES = H // K_PASS
CHUNK = 1024
FF_CHUNKS = FF // CHUNK
EPS = 1e-7
HV = (256, 256)
G1V = (512, 0)

FIRST_ROUND = (2, 3, 5)
GELU_DELAY = 4

FLOPS = 2 * TOKENS * H * (H + FF)


def tile_disentangledattention_pb_kernel(
    tc, head_context, h, Wo, bo, ln1_g, ln1_b, Wi, bi, out_0, out_1
):
    nc = tc.nc
    h_rows = h.flatten_outer_dims()
    a_rows = out_0.flatten_outer_dims()
    f_rows = out_1.flatten_outer_dims()

    with ExitStack() as ctx:
        consts = ctx.enter_context(tc.tile_pool(name="consts", bufs=1))
        keep = ctx.enter_context(tc.tile_pool(name="keep", bufs=1))
        acts = ctx.enter_context(tc.tile_pool(name="acts", bufs=5))
        raws = ctx.enter_context(tc.tile_pool(name="raws", bufs=5))
        stage = ctx.enter_context(tc.tile_pool(name="stage", bufs=2))
        small = ctx.enter_context(tc.tile_pool(name="small", bufs=2))
        mid = ctx.enter_context(tc.tile_pool(name="mid", bufs=3))
        stats = ctx.enter_context(tc.tile_pool(name="stats", bufs=4))
        fpool = ctx.enter_context(tc.tile_pool(name="fpool", bufs=5))
        outs = ctx.enter_context(tc.tile_pool(name="outs", bufs=6))
        psum_mm = ctx.enter_context(tc.psum_pool(name="psum_mm", bufs=4))
        psum_tr = ctx.enter_context(tc.psum_pool(name="psum_tr", bufs=2))
        psum_rows = ctx.enter_context(tc.psum_pool(name="psum_rows", bufs=1))

        ident_f32 = consts.tile([P, P], F32)
        make_identity(nc, ident_f32[:])
        ident_bf16 = consts.tile([P, P], BF16)
        make_identity(nc, ident_bf16[:])
        ones_bf16 = consts.tile([P, P], BF16)
        nc.vector.memset(ones_bf16[:], 1.0)
        minus_half = consts.tile([P, 1], F32)
        nc.vector.memset(minus_half[:], -0.5)
        warm = consts.tile([P, 1], F32)
        nc.scalar.activation(out=warm[:], in_=minus_half[:], func=ACT.Gelu)

        rows = consts.tile([P, 3 * H], BF16)
        nc.vector.memset(rows[:].bitcast(I32), 0)
        first = 0
        for vec in (bo, ln1_g, ln1_b):
            width = vec.shape[0]
            nc.scalar.dma_start(
                out=rows[0:1, first : first + width],
                in_=vec.rearrange("(o n) -> o n", o=1),
            )
            first += width
        bo_rows = rows[:, 0:H]
        bi_bc = consts.tile([P, FF], BF16)

        wo_codes = keep.tile([P, PASSES, H], U32, align_bytes=64)
        wo_scales = keep.tile([P, PASSES, H], U8, align_bytes=64)
        wi_codes = keep.tile([P, PASSES, FF], U32, align_bytes=64)
        wi_scales = keep.tile([P, PASSES, FF], U8, align_bytes=64)
        c_codes = keep.tile([P, TOK_TILES, PASSES, P], U32, align_bytes=64)
        c_scales = keep.tile([P, TOK_TILES, PASSES, P], U8, align_bytes=64)
        a_codes = keep.tile([P, TOK_TILES, PASSES, P], U32, align_bytes=64)
        a_scales = keep.tile([P, TOK_TILES, PASSES, P], U8, align_bytes=64)

        def load_wo(g):
            raw = raws.tile([P, PACK, CHUNK], BF16, tag="raw")
            if g == 0:
                for c0 in range(0, CHUNK, BANK):
                    for u in range(2):
                        k0 = u * 2 * P
                        nc.sync.dma_start(
                            out=raw[:, 2 * u : 2 * u + 2, c0 : c0 + BANK],
                            in_=Wo[k0 : k0 + 2 * P, c0 : c0 + BANK].rearrange("(q e) c -> q e c", e=2),
                        )
            else:
                nc.sync.dma_start(
                    out=raw[:].rearrange("q (u e) c -> q u (e c)", u=2),
                    in_=Wo[g * K_PASS : (g + 1) * K_PASS, :].rearrange("(u q e) c -> q u (e c)", u=2, e=2),
                )
            return raw

        def load_wi(chunk):
            j, g = divmod(chunk, PASSES)
            raw = raws.tile([P, PACK, CHUNK], BF16, tag="raw")
            nc.sync.dma_start(
                out=raw[:],
                in_=Wi[g * K_PASS : (g + 1) * K_PASS, j * CHUNK : (j + 1) * CHUNK].rearrange(
                    "(t p) c -> p t c", p=P
                ),
            )
            return raw

        def regroup(raw, half, by_vector):
            grouped = stage.tile([P, BANK, PACK], BF16, tag="grouped%d" % half, align_bytes=64)
            raw_half = raw[:, :, half * BANK : (half + 1) * BANK]
            for copy, c0, c1 in (
                (nc.vector.tensor_copy, 0, by_vector),
                (nc.scalar.copy, by_vector, BANK),
            ):
                if c0 < c1:
                    copy(
                        out=grouped[:, c0:c1, :].rearrange("p (c i) t -> p c t i", i=8),
                        in_=raw_half[:, :, c0:c1].rearrange("p t (c i) -> p c t i", i=8),
                    )
            return grouped

        def quantise(grouped, half, codes, scales):
            cols = slice(half * BANK, (half + 1) * BANK)
            nc.vector.quantize_mx(
                out=codes[:, cols].bitcast(FP8X4),
                scales=scales[:, cols],
                in_=grouped[:].rearrange("p w t -> p (w t)"),
            )

        def quantise_wi(grouped, half, chunk):
            j, g = divmod(chunk, PASSES)
            cols = slice(j * CHUNK, (j + 1) * CHUNK)
            quantise(grouped, half, wi_codes[:, g, cols], wi_scales[:, g, cols])

        c_raws = {}
        h_raws = {}
        c_groupeds = {}
        a_groupeds = {}
        u_tiles = {}
        a_tiles = {}
        negmeans = {}
        rstds = {}

        def load_tokens(i):
            b = i // (TOK_TILES // 2)
            s0 = (i % (TOK_TILES // 2)) * P
            c_raw = acts.tile([P, H], BF16)
            nc.sync.dma_start(
                out=c_raw[:].rearrange("s (n d) -> s n d", n=HEADS),
                in_=head_context[b, :, s0 : s0 + P, :].rearrange("n s d -> s n d"),
            )
            c_raws[i] = c_raw
            h_raw = acts.tile([P, H], BF16)
            nc.sync.dma_start(out=h_raw[:], in_=h_rows[i * P : (i + 1) * P, :])
            h_raws[i] = h_raw

        def c_in(i):
            c_words = c_raws[i][:].bitcast(F32)
            ct = psum_tr.tile([P, PACK, P], F32, tag="tr")
            for w in range(PACK):
                nc.tensor.transpose(ct[:, w, :], c_words[:, w * P : (w + 1) * P], ident_f32[:])
            c_grouped = small.tile([P, H], BF16, align_bytes=64)
            nc.scalar.copy(
                out=c_grouped[:].bitcast(F32).rearrange("q (g r u) -> q g r u", g=PASSES, u=2),
                in_=ct[:].rearrange("q (g u) r -> q g r u", u=2),
            )
            c_groupeds[i] = c_grouped

        def residual_in(i):
            u = mid.tile([P, H], F32)
            for n in range(H // BANK):
                cols = slice(n * BANK, (n + 1) * BANK)
                hb = psum_mm.tile([P, BANK], F32, tag="mm")
                nc.tensor.matmul(hb[:], lhsT=ident_bf16[:], rhs=h_raws[i][:, cols], start=True, stop=False)
                nc.tensor.matmul(hb[:], lhsT=ones_bf16[:], rhs=bo_rows[:, cols], start=False, stop=True)
                nc.scalar.copy(out=u[:, cols], in_=hb[:])
            u_tiles[i] = u

        def quantise_c(i):
            nc.vector.quantize_mx(
                out=c_codes[:, i].rearrange("q g r -> q (g r)").bitcast(FP8X4),
                scales=c_scales[:, i].rearrange("q g r -> q (g r)"),
                in_=c_groupeds[i][:],
            )

        def project(i):
            u = u_tiles[i]
            sums = stats.tile([P, H // BANK], F32)
            for n in range(H // BANK):
                cols = slice(n * BANK, (n + 1) * BANK)
                y = psum_mm.tile([P, BANK], F32, tag="mm")
                for g in range(PASSES):
                    nc.tensor.matmul_mx(
                        out=y[:],
                        lhsT=c_codes[:, i, g, :].bitcast(FP8X4),
                        lhsT_scale=c_scales[:, i, g, :],
                        rhs=wo_codes[:, g, cols].bitcast(FP8X4),
                        rhs_scale=wo_scales[:, g, cols],
                        start=(g == 0),
                        stop=(g == PASSES - 1),
                    )
                nc.vector.scalar_tensor_tensor(
                    out=u[:, cols], in0=y[:], scalar=1.0, in1=u[:, cols],
                    op0=ALU.mult, op1=ALU.add, accum_out=sums[:, n : n + 1],
                )
            negmean = stats.tile([P, 1], F32)
            nc.vector.tensor_scalar(
                out=negmean[:], in0=sums[:, 0:1], scalar1=sums[:, 1:2], scalar2=-1.0 / H,
                op0=ALU.add, op1=ALU.mult,
            )
            negmeans[i] = negmean

        def variance(i):
            squares = small.tile([P, H], BF16)
            ssq = stats.tile([P, 1], F32)
            nc.scalar.activation(
                out=squares[:], in_=u_tiles[i][:], func=ACT.Square, bias=negmeans[i][:, 0:1],
                accum_out=ssq[:],
            )
            var_eps = stats.tile([P, 1], F32)
            nc.gpsimd.tensor_scalar(
                out=var_eps[:], in0=ssq[:], scalar1=1.0 / H, scalar2=EPS, op0=ALU.mult, op1=ALU.add,
            )
            rstd = stats.tile([P, 1], F32)
            nc.gpsimd.tensor_tensor(out=rstd[:], in0=var_eps[:], in1=minus_half[:], op=ALU.pow)
            rstds[i] = rstd

        def centre(i):
            a_t = mid.tile([P, H], F32)
            nc.vector.scalar_tensor_tensor(
                out=a_t[:], in0=u_tiles[i][:], scalar=negmeans[i][:, 0:1], in1=g_psum[:],
                op0=ALU.add, op1=ALU.mult,
            )
            a_tiles[i] = a_t

        def scale_shift(i):
            a_t = a_tiles[i]
            nc.vector.scalar_tensor_tensor(
                out=a_t[:], in0=a_t[:], scalar=rstds[i][:, 0:1], in1=b_psum[:], op0=ALU.mult, op1=ALU.add,
            )
            nc.sync.dma_start(out=a_rows[i * P : (i + 1) * P, :], in_=a_t[:])

        def a_transposed(i):
            a_grouped = small.tile([P, PASSES, P, PACK], BF16, align_bytes=64)
            for g in range(PASSES):
                at = psum_tr.tile([P, PACK, P], F32, tag="tr")
                for t in range(PACK):
                    k0 = g * K_PASS + t * P
                    nc.tensor.transpose(at[:, t, :], a_tiles[i][:, k0 : k0 + P], ident_f32[:])
                nc.scalar.copy(out=a_grouped[:, g], in_=at[:].rearrange("p t r -> p r t"))
            a_groupeds[i] = a_grouped

        def quantise_a(i):
            nc.vector.quantize_mx(
                out=a_codes[:, i].rearrange("p g r -> p (g r)").bitcast(FP8X4),
                scales=a_scales[:, i].rearrange("p g r -> p (g r)"),
                in_=a_groupeds[i][:].rearrange("p g r t -> p (g r t)"),
            )

        def back_sums(i, first, width):
            f_t = fpool.tile([P, CHUNK], F32)
            for n in range(width // BANK):
                cols = slice(first + n * BANK, first + (n + 1) * BANK)
                acc = psum_mm.tile([P, BANK], F32, tag="mm")
                for g in range(PASSES):
                    nc.tensor.matmul_mx(
                        out=acc[:],
                        lhsT=a_codes[:, i, g, :].bitcast(FP8X4),
                        lhsT_scale=a_scales[:, i, g, :],
                        rhs=wi_codes[:, g, cols].bitcast(FP8X4),
                        rhs_scale=wi_scales[:, g, cols],
                        start=(g == 0),
                        stop=(g == PASSES - 1),
                    )
                nc.vector.tensor_tensor(
                    out=f_t[:, n * BANK : (n + 1) * BANK], in0=acc[:], in1=bi_bc[:, cols], op=ALU.add,
                )
            return f_t

        sums_out = []
        gelus_out = []

        def back(i, first, width):
            sums_out.append((i, first, width, back_sums(i, first, width)))
            if len(sums_out) - len(gelus_out) > GELU_DELAY:
                gelu(*sums_out[len(gelus_out)])

        def gelu(i, first, width, f_t):
            gelus_out.append(i)
            f_out = outs.tile([P, CHUNK], F32)
            nc.scalar.activation(out=f_out[:, 0:width], in_=f_t[:, 0:width], func=ACT.Gelu)
            nc.sync.dma_start(
                out=f_rows[i * P : (i + 1) * P, first : first + width], in_=f_out[:, 0:width]
            )

        def spread(bank, first):
            for n in range(2):
                cols = slice(first + n * BANK, first + (n + 1) * BANK)
                nc.tensor.matmul(
                    bank[:, n * BANK : (n + 1) * BANK],
                    lhsT=ones_bf16[:],
                    rhs=rows[:, cols],
                    start=True,
                    stop=True,
                )

        g_psum = psum_rows.tile([P, H], BF16)
        b_psum = psum_rows.tile([P, H], BF16)

        wo_raws = {}
        wi_raws = {}
        for g in range(PASSES):
            wo_raws[g] = load_wo(g)
        for i in range(3):
            load_tokens(i)
            wi_raws[i] = load_wi(i)

        wo_grouped = {}
        for half in range(2):
            wo_grouped[0, half] = regroup(wo_raws[0], half, HV[half])
        load_tokens(3)
        wi_raws[3] = load_wi(3)
        nc.sync.dma_start(out=bi_bc[:], in_=bi.partition_broadcast(P))
        quantise(wo_grouped[0, 0], 0, wo_codes[:, 0, :], wo_scales[:, 0, :])
        for half in range(2):
            wo_grouped[1, half] = regroup(wo_raws[1], half, G1V[half])
        wi_raws[4] = load_wi(4)
        load_tokens(4)
        quantise(wo_grouped[0, 1], 1, wo_codes[:, 0, :], wo_scales[:, 0, :])
        quantise(wo_grouped[1, 0], 0, wo_codes[:, 1, :], wo_scales[:, 1, :])
        c_in(0)
        residual_in(0)
        load_tokens(5)
        quantise(wo_grouped[1, 1], 1, wo_codes[:, 1, :], wo_scales[:, 1, :])
        quantise_c(0)
        spread(g_psum, H)
        spread(b_psum, 2 * H)

        def prepare(chunk):
            raw = wi_raws[chunk]
            half_1 = regroup(raw, 1, 0)
            half_0 = regroup(raw, 0, BANK - P if chunk >= 3 else BANK)
            if chunk == 0:
                wi_raws[5] = load_wi(5)
            return half_0, half_1

        def quantise_chunk(chunk, halves):
            for half in range(2):
                quantise_wi(halves[half], half, chunk)

        pieces = {}
        for j in range(FF_CHUNKS):
            for d in range(TOK_TILES):
                pieces.setdefault(max(d + 2, FIRST_ROUND[j] + (d + 1) // 2), []).append((d, j))
        chunks = {0: [0, 1], 1: [2], 2: [3], 3: [4], 4: [5]}

        for r in range(TOK_TILES + 2):
            comes_in = r + 1 < TOK_TILES
            projects = r < TOK_TILES
            normalises = 0 <= r - 1 < TOK_TILES
            going_out = pieces.get(r, [])
            new_chunks = chunks.get(r, [])

            for chunk in new_chunks[0:1]:
                halves = prepare(chunk)
            if normalises:
                scale_shift(r - 1)
            if projects:
                project(r)
            if comes_in:
                residual_in(r + 1)
                c_in(r + 1)
                if r + 6 < TOK_TILES:
                    load_tokens(r + 6)
            if projects:
                variance(r)
                centre(r)
            for d, j in going_out[0:1]:
                back(d, j * CHUNK, CHUNK)
            if normalises:
                a_transposed(r - 1)
            for d, j in going_out[1:2]:
                back(d, j * CHUNK, CHUNK)
            for chunk in new_chunks[0:1]:
                quantise_chunk(chunk, halves)
            if normalises:
                quantise_a(r - 1)
            if comes_in:
                quantise_c(r + 1)
            for d, j in going_out[2:]:
                width = BANK if (d, j) == (TOK_TILES - 1, FF_CHUNKS - 1) else CHUNK
                for first in range(j * CHUNK, (j + 1) * CHUNK, width):
                    back(d, first, width)
            for chunk in new_chunks[1:]:
                quantise_chunk(chunk, prepare(chunk))
        for piece in sums_out[len(gelus_out) :]:
            gelu(*piece)
